import numpy as np
import ml_dtypes


def mxq(x, axis, fmt="e4m3"):
    dtype, down = {"e4m3": (ml_dtypes.float8_e4m3fn, 7), "e5m2": (ml_dtypes.float8_e5m2, 14)}[fmt]
    v = np.moveaxis(np.asarray(x, np.float32).astype(ml_dtypes.bfloat16).astype(np.float64), axis, -1)
    blocks = v.reshape(v.shape[:-1] + (-1, 32))
    amax = np.abs(blocks).max(-1, keepdims=True)
    byte = np.maximum(np.where(amax > 0, np.frexp(amax)[1] - 1 + 127, 0) - down, 1)
    scale = np.exp2(byte - 127.0)
    codes = (blocks / scale).astype(np.float32).astype(dtype).astype(np.float64)
    return np.moveaxis((codes * scale).reshape(v.shape), -1, axis)


WIDE = False


def mx_kscale(k):
    if not WIDE:
        return np.ones(k)
    levels = np.array([10, -10, 5, -5, 0])
    a = np.random.permutation(np.resize(levels, k // 512 * 4)).reshape(k // 512, 4)
    idx = np.arange(k)
    return np.exp2(a[idx // 512, idx % 128 // 32])


BF16 = ml_dtypes.bfloat16


def bf(x):
    return np.asarray(x, np.float32).astype(BF16)


def f64(x):
    return np.asarray(x).astype(np.float64)


B, CIN, CMID, C4, C8, COUT, T, H, W = 2, 128, 16384, 256, 128, 128, 4, 16, 8
S = T * H * W


def setup_inputs():
    s = mx_kscale(CMID)
    h_add = np.maximum(np.random.standard_normal((B, CMID, S)) * np.sqrt(2.0), 0.0)
    h_occ = np.maximum(np.random.standard_normal((B, C8, S)) * np.sqrt(2.0), 0.0)
    return {"h_add": bf(h_add * s[None, :, None]),
            "w_add2": bf(np.random.standard_normal((CIN, CMID)) * np.sqrt(2.0 / CMID) / s[None, :]),
            "b_add2": bf(np.random.standard_normal(CIN) * 0.3),
            "h_occ": bf(h_occ),
            "w_occ3": bf(np.random.standard_normal((COUT, C8)) / np.sqrt(C8))}


def reference(h_add, w_add2, b_add2, h_occ, w_occ3):
    feat = (mxq(f64(w_add2), 1, "e4m3") @ mxq(f64(h_add), 1, "e4m3")) + f64(b_add2)[None, :, None]
    occ = np.abs(f64(w_occ3) @ f64(h_occ))
    return (mxq(occ, 2, "e4m3") @ mxq(feat, 2, "e4m3").transpose(0, 2, 1)) / S

@@ -1,0 +1,228 @@
+from contextlib import ExitStack
+
+import concourse.mybir as mybir
+from concourse.masks import make_identity
+
+F32 = mybir.dt.float32
+BF16 = mybir.dt.bfloat16
+U32 = mybir.dt.uint32
+U8 = mybir.dt.uint8
+FP8X4 = mybir.dt.float8_e4m3fn_x4
+
+B, CIN, CMID, C8, COUT, S = 2, 128, 16384, 128, 128, 512
+
+P = 128
+PACK = 4
+K_PASS = P * PACK
+PASSES = CMID // K_PASS
+V_TILES = S // P
+
+PAIR = 2
+PAIRS = PASSES // PAIR
+W_PASSES = 8
+PAIRS_PER_W_LOAD = W_PASSES // PAIR
+QUANT_LAG = 2
+
+FLOPS = 2 * B * S * (CIN * CMID + COUT * C8 + COUT * CIN)
+
+
+def tile_occurrencepool_pa_k_kernel(tc, h_add, w_add2, b_add2, h_occ, w_occ3, out):
+    nc = tc.nc
+    with ExitStack() as ctx:
+        const = ctx.enter_context(tc.tile_pool(name="const", bufs=1))
+        w_loads = ctx.enter_context(tc.tile_pool(name="w_loads", bufs=2))
+        w_stage = ctx.enter_context(tc.tile_pool(name="w_stage", bufs=3))
+        h_loads = ctx.enter_context(tc.tile_pool(name="h_loads", bufs=8))
+        h_groups = ctx.enter_context(tc.tile_pool(name="h_groups", bufs=QUANT_LAG + 2))
+        h_stage = ctx.enter_context(tc.tile_pool(name="h_stage", bufs=3))
+        pooling = ctx.enter_context(tc.tile_pool(name="pooling", bufs=2))
+        psum_feat = ctx.enter_context(tc.psum_pool(name="psum_feat", bufs=1))
+        psum_wt = ctx.enter_context(tc.psum_pool(name="psum_wt", bufs=2))
+        psum_small = ctx.enter_context(tc.psum_pool(name="psum_small", bufs=2))
+        ctx.enter_context(tc.manual_schedule())
+
+        ident_bf16 = const.tile([P, P], BF16)
+        make_identity(nc, ident_bf16[:])
+        ident_f32 = const.tile([P, P], F32)
+        make_identity(nc, ident_f32[:])
+        ones = const.tile([P, P], BF16)
+        nc.vector.memset(ones[:], 1.0)
+        bias_row = const.tile([P, CIN], BF16)
+        nc.vector.memset(bias_row[:], 0.0)
+
+        w_occ_sb = const.tile([COUT, C8], BF16)
+        nc.sync.dma_start(out=w_occ_sb[:], in_=w_occ3)
+        h_occ_sb = const.tile([C8, B, S], BF16)
+        nc.sync.dma_start(out=h_occ_sb[:], in_=h_occ.rearrange("b c v -> c b v"))
+        nc.sync.dma_start(out=bias_row[0:1, :], in_=b_add2.unsqueeze(0))
+
+        bias_ps = psum_small.tile([P, CIN], F32, tag="small")
+        nc.tensor.matmul(bias_ps[:], lhsT=ones[:], rhs=bias_row[:], start=True, stop=True)
+        bias_all = const.tile([P, CIN], F32)
+        nc.vector.tensor_copy(out=bias_all[:], in_=bias_ps[:])
+
+        w_occ_ps = psum_small.tile([C8, COUT], BF16, tag="small")
+        nc.tensor.transpose(w_occ_ps[:], w_occ_sb[:], ident_bf16[:])
+        w_occ_t = const.tile([C8, COUT], BF16)
+        nc.vector.tensor_copy(out=w_occ_t[:], in_=w_occ_ps[:])
+
+        table_warmer = const.tile([P, 1], F32)
+        nc.scalar.activation(out=table_warmer[:], in_=ones[:, 0:1], func=mybir.ActivationFunctionType.Abs)
+
+        occ_grouped = const.tile([P, B, COUT, PACK], BF16, align_bytes=64)
+
+        def occurrence_maps(b):
+            occ_ps = psum_small.tile([P, V_TILES, COUT], F32, tag="small")
+            for t in range(V_TILES):
+                nc.tensor.matmul(
+                    occ_ps[:, t, :],
+                    lhsT=h_occ_sb[:, b, t * P : (t + 1) * P],
+                    rhs=w_occ_t[:],
+                    start=True,
+                    stop=True,
+                )
+            nc.scalar.activation(
+                out=occ_grouped[:, b],
+                in_=occ_ps[:].rearrange("p t o -> p o t"),
+                func=mybir.ActivationFunctionType.Abs,
+            )
+
+        w_codes = const.tile([P, PASSES * CIN], U32, align_bytes=64)
+        w_scales = const.tile([P, PASSES * CIN], U8, align_bytes=64)
+
+        def load_w(first_pass):
+            w_raw = w_loads.tile([CIN, W_PASSES * K_PASS], BF16)
+            k0 = first_pass * K_PASS
+            nc.sync.dma_start(out=w_raw[:], in_=w_add2[:, k0 : k0 + W_PASSES * K_PASS])
+            return w_raw[:].bitcast(F32).rearrange("c (g p u) -> c g u p", p=P, u=2)
+
+        def transpose_w_pair(w_words, g0):
+            w_bank = psum_wt.tile([P, PAIR, 2, CIN], F32)
+            for g in range(PAIR):
+                for u in range(2):
+                    nc.tensor.transpose(w_bank[:, g, u, :], w_words[:, g0 + g, u, :], ident_f32[:])
+            return w_bank
+
+        def regroup_w_pair(w_bank):
+            w_grouped = w_stage.tile([P, PAIR * CIN * PACK], BF16, align_bytes=64)
+            nc.scalar.copy(
+                out=w_grouped[:].bitcast(F32).rearrange("p (g c u) -> p g c u", c=CIN, u=2),
+                in_=w_bank[:].rearrange("p g u c -> p g c u"),
+            )
+            return w_grouped
+
+        def quantise_w_pair(pair, w_grouped):
+            cols = slice(pair * PAIR * CIN, (pair + 1) * PAIR * CIN)
+            nc.vector.quantize_mx(
+                out=w_codes[:, cols].bitcast(FP8X4), scales=w_scales[:, cols], in_=w_grouped[:]
+            )
+
+        def regroup(copy, grouped, rows):
+            copy(
+                out=grouped.rearrange("p (c i) t -> p c t i", i=4),
+                in_=rows.rearrange("p t (c i) -> p c t i", i=4),
+            )
+
+        def load_and_regroup(b, pair):
+            h_raw = h_loads.tile([P, PAIR, PACK, S], BF16)
+            k0 = pair * PAIR * K_PASS
+            nc.sync.dma_start(
+                out=h_raw[:],
+                in_=h_add[b, k0 : k0 + PAIR * K_PASS, :].rearrange("(g p t) v -> p g t v", p=P, t=PACK),
+            )
+            h_grouped = h_groups.tile([P, PAIR, S, PACK], BF16, align_bytes=64)
+            regroup(nc.vector.tensor_copy, h_grouped[:, 0], h_raw[:, 0])
+            regroup(nc.scalar.copy, h_grouped[:, 1], h_raw[:, 1])
+            return h_grouped
+
+        def quantise_and_multiply(pair, h_grouped, feat_ps):
+            h_codes = h_stage.tile([P, PAIR * S], U32, align_bytes=64)
+            h_scales = h_stage.tile([P, PAIR * S], U8, align_bytes=64)
+            nc.vector.quantize_mx(
+                out=h_codes[:].bitcast(FP8X4),
+                scales=h_scales[:],
+                in_=h_grouped[:].rearrange("p g v t -> p (g v t)"),
+            )
+            for g in range(PAIR):
+                k_pass = pair * PAIR + g
+                w_cols = slice(k_pass * CIN, (k_pass + 1) * CIN)
+                for j in range(V_TILES):
+                    v_cols = slice(g * S + j * P, g * S + (j + 1) * P)
+                    nc.tensor.matmul_mx(
+                        out=feat_ps[j][:],
+                        lhsT=h_codes[:, v_cols].bitcast(FP8X4),
+                        lhsT_scale=h_scales[:, v_cols],
+                        rhs=w_codes[:, w_cols].bitcast(FP8X4),
+                        rhs_scale=w_scales[:, w_cols],
+                        start=(k_pass == 0),
+                        stop=(k_pass == PASSES - 1),
+                    )
+
+        result = const.tile([COUT, B, CIN], F32)
+
+        def pool_sample(b, feat_ps):
+            occ_codes = pooling.tile([P, COUT], U32, align_bytes=64)
+            occ_scales = pooling.tile([P, COUT], U8, align_bytes=64)
+            nc.vector.quantize_mx(
+                out=occ_codes[:].bitcast(FP8X4),
+                scales=occ_scales[:],
+                in_=occ_grouped[:, b].rearrange("p o t -> p (o t)"),
+            )
+            feat_rows = pooling.tile([P, V_TILES, CIN], BF16)
+            for j in range(V_TILES):
+                nc.vector.tensor_tensor(
+                    out=feat_rows[:, j, :], in0=feat_ps[j][:], in1=bias_all[:], op=mybir.AluOpType.add
+                )
+            feat_grouped = pooling.tile([P, CIN, PACK], BF16, align_bytes=64)
+            nc.vector.tensor_copy(out=feat_grouped[:], in_=feat_rows[:].rearrange("p t c -> p c t"))
+            feat_codes = pooling.tile([P, CIN], U32, align_bytes=64)
+            feat_scales = pooling.tile([P, CIN], U8, align_bytes=64)
+            nc.vector.quantize_mx(
+                out=feat_codes[:].bitcast(FP8X4),
+                scales=feat_scales[:],
+                in_=feat_grouped[:].rearrange("p c t -> p (c t)"),
+            )
+            out_ps = psum_small.tile([COUT, CIN], F32, tag="small")
+            nc.tensor.matmul_mx(
+                out=out_ps[:],
+                lhsT=occ_codes[:].bitcast(FP8X4),
+                lhsT_scale=occ_scales[:],
+                rhs=feat_codes[:].bitcast(FP8X4),
+                rhs_scale=feat_scales[:],
+                start=True,
+                stop=True,
+            )
+            nc.scalar.mul(out=result[:, b, :], in_=out_ps[:], mul=1.0 / S)
+
+        pairs = [(b, pair) for b in range(B) for pair in range(PAIRS)]
+        h_grouped = {}
+        w_banks = {}
+        w_grouped = {}
+        feat_ps = {}
+        for turn in range(len(pairs) + QUANT_LAG + 1):
+            if turn < len(pairs):
+                h_grouped[turn] = load_and_regroup(*pairs[turn])
+            if turn == 0:
+                for b in range(B):
+                    occurrence_maps(b)
+            if turn - 1 in w_banks:
+                w_grouped[turn - 1] = regroup_w_pair(w_banks[turn - 1])
+
+            multiplied = turn - QUANT_LAG
+            if multiplied in w_grouped:
+                quantise_w_pair(multiplied, w_grouped[multiplied])
+            if multiplied >= PAIRS and multiplied % PAIRS == 0:
+                b = multiplied // PAIRS - 1
+                pool_sample(b, feat_ps[b])
+            if 0 <= multiplied < len(pairs):
+                b, pair = pairs[multiplied]
+                if pair == 0:
+                    feat_ps[b] = [psum_feat.tile([P, CIN], F32, name="feat_ps%d" % j) for j in range(V_TILES)]
+                quantise_and_multiply(pair, h_grouped[multiplied], feat_ps[b])
+
+            if turn < PAIRS:
+                if turn % PAIRS_PER_W_LOAD == 0:
+                    w_words = load_w(turn * PAIR)
+                w_banks[turn] = transpose_w_pair(w_words, turn % PAIRS_PER_W_LOAD * PAIR)
+
+        nc.sync.dma_start(out=out.rearrange("b o c -> o b c"), in_=result[:])

@@ -19,9 +19,6 @@ V_TILES = S // P
 
 PAIR = 2
 PAIRS = PASSES // PAIR
-W_PASSES = 8
-PAIRS_PER_W_LOAD = W_PASSES // PAIR
-QUANT_LAG = 2
 
 FLOPS = 2 * B * S * (CIN * CMID + COUT * C8 + COUT * CIN)
 
@@ -30,11 +27,11 @@ def tile_occurrencepool_pa_k_kernel(tc, h_add, w_add2, b_add2, h_occ, w_occ3, ou
     nc = tc.nc
     with ExitStack() as ctx:
         const = ctx.enter_context(tc.tile_pool(name="const", bufs=1))
-        w_loads = ctx.enter_context(tc.tile_pool(name="w_loads", bufs=2))
+        w_loads = ctx.enter_context(tc.tile_pool(name="w_loads", bufs=4))
         w_stage = ctx.enter_context(tc.tile_pool(name="w_stage", bufs=3))
-        h_loads = ctx.enter_context(tc.tile_pool(name="h_loads", bufs=8))
-        h_groups = ctx.enter_context(tc.tile_pool(name="h_groups", bufs=QUANT_LAG + 2))
-        h_stage = ctx.enter_context(tc.tile_pool(name="h_stage", bufs=3))
+        h_loads = ctx.enter_context(tc.tile_pool(name="h_loads", bufs=16))
+        h_groups = ctx.enter_context(tc.tile_pool(name="h_groups", bufs=4))
+        h_quantised = ctx.enter_context(tc.tile_pool(name="h_quantised", bufs=4))
         pooling = ctx.enter_context(tc.tile_pool(name="pooling", bufs=2))
         psum_feat = ctx.enter_context(tc.psum_pool(name="psum_feat", bufs=1))
         psum_wt = ctx.enter_context(tc.psum_pool(name="psum_wt", bufs=2))
@@ -90,17 +87,15 @@ def tile_occurrencepool_pa_k_kernel(tc, h_add, w_add2, b_add2, h_occ, w_occ3, ou
         w_codes = const.tile([P, PASSES * CIN], U32, align_bytes=64)
         w_scales = const.tile([P, PASSES * CIN], U8, align_bytes=64)
 
-        def load_w(first_pass):
-            w_raw = w_loads.tile([CIN, W_PASSES * K_PASS], BF16)
-            k0 = first_pass * K_PASS
-            nc.sync.dma_start(out=w_raw[:], in_=w_add2[:, k0 : k0 + W_PASSES * K_PASS])
-            return w_raw[:].bitcast(F32).rearrange("c (g p u) -> c g u p", p=P, u=2)
-
-        def transpose_w_pair(w_words, g0):
+        def load_and_transpose_w_pair(pair):
+            w_raw = w_loads.tile([CIN, PAIR * K_PASS], BF16)
+            k0 = pair * PAIR * K_PASS
+            nc.sync.dma_start(out=w_raw[:], in_=w_add2[:, k0 : k0 + PAIR * K_PASS])
+            w_words = w_raw[:].bitcast(F32).rearrange("c (g p u) -> c g u p", p=P, u=2)
             w_bank = psum_wt.tile([P, PAIR, 2, CIN], F32)
             for g in range(PAIR):
                 for u in range(2):
-                    nc.tensor.transpose(w_bank[:, g, u, :], w_words[:, g0 + g, u, :], ident_f32[:])
+                    nc.tensor.transpose(w_bank[:, g, u, :], w_words[:, g, u, :], ident_f32[:])
             return w_bank
 
         def regroup_w_pair(w_bank):
@@ -123,30 +118,32 @@ def tile_occurrencepool_pa_k_kernel(tc, h_add, w_add2, b_add2, h_occ, w_occ3, ou
                 in_=rows.rearrange("p t (c i) -> p c t i", i=4),
             )
 
-        def load_and_regroup(b, pair):
-            h_raw = h_loads.tile([P, PAIR, PACK, S], BF16)
-            k0 = pair * PAIR * K_PASS
-            nc.sync.dma_start(
-                out=h_raw[:],
-                in_=h_add[b, k0 : k0 + PAIR * K_PASS, :].rearrange("(g p t) v -> p g t v", p=P, t=PACK),
-            )
+        def load_and_regroup(b, pair, copies):
             h_grouped = h_groups.tile([P, PAIR, S, PACK], BF16, align_bytes=64)
-            regroup(nc.vector.tensor_copy, h_grouped[:, 0], h_raw[:, 0])
-            regroup(nc.scalar.copy, h_grouped[:, 1], h_raw[:, 1])
+            for g, copy in enumerate(copies):
+                h_raw = h_loads.tile([P, PACK, S], BF16)
+                k0 = (pair * PAIR + g) * K_PASS
+                nc.sync.dma_start(
+                    out=h_raw[:], in_=h_add[b, k0 : k0 + K_PASS, :].rearrange("(p t) v -> p t v", t=PACK)
+                )
+                regroup(copy, h_grouped[:, g], h_raw[:])
             return h_grouped
 
-        def quantise_and_multiply(pair, h_grouped, feat_ps):
-            h_codes = h_stage.tile([P, PAIR * S], U32, align_bytes=64)
-            h_scales = h_stage.tile([P, PAIR * S], U8, align_bytes=64)
+        def quantise_h_pair(h_grouped):
+            h_codes = h_quantised.tile([P, PAIR * S], U32, align_bytes=64)
+            h_scales = h_quantised.tile([P, PAIR * S], U8, align_bytes=64)
             nc.vector.quantize_mx(
                 out=h_codes[:].bitcast(FP8X4),
                 scales=h_scales[:],
                 in_=h_grouped[:].rearrange("p g v t -> p (g v t)"),
             )
-            for g in range(PAIR):
-                k_pass = pair * PAIR + g
-                w_cols = slice(k_pass * CIN, (k_pass + 1) * CIN)
-                for j in range(V_TILES):
+            return h_codes, h_scales
+
+        def multiply_pair(pair, h_codes, h_scales, feat_ps):
+            for j in range(V_TILES):
+                for g in range(PAIR):
+                    k_pass = pair * PAIR + g
+                    w_cols = slice(k_pass * CIN, (k_pass + 1) * CIN)
                     v_cols = slice(g * S + j * P, g * S + (j + 1) * P)
                     nc.tensor.matmul_mx(
                         out=feat_ps[j][:],
@@ -195,34 +192,37 @@ def tile_occurrencepool_pa_k_kernel(tc, h_add, w_add2, b_add2, h_occ, w_occ3, ou
             nc.scalar.mul(out=result[:, b, :], in_=out_ps[:], mul=1.0 / S)
 
         pairs = [(b, pair) for b in range(B) for pair in range(PAIRS)]
-        h_grouped = {}
-        w_banks = {}
-        w_grouped = {}
-        feat_ps = {}
-        for turn in range(len(pairs) + QUANT_LAG + 1):
-            if turn < len(pairs):
-                h_grouped[turn] = load_and_regroup(*pairs[turn])
+        last = len(pairs) - 1
+        regrouped = {}
+        quantised = {}
+        w_transposed = {}
+        w_regrouped = {}
+        feat_sums = {}
+        for turn in range(len(pairs) + 3):
+            if turn <= last:
+                first_copy = nc.vector.tensor_copy if turn == 0 else nc.scalar.copy
+                second_copy = nc.scalar.copy if turn == last else nc.vector.tensor_copy
+                regrouped[turn] = load_and_regroup(*pairs[turn], (first_copy, second_copy))
             if turn == 0:
                 for b in range(B):
                     occurrence_maps(b)
-            if turn - 1 in w_banks:
-                w_grouped[turn - 1] = regroup_w_pair(w_banks[turn - 1])
+            if turn - 1 in w_transposed:
+                w_regrouped[turn - 1] = regroup_w_pair(w_transposed[turn - 1])
+            if turn - 1 in regrouped:
+                quantised[turn - 1] = quantise_h_pair(regrouped[turn - 1])
+            if turn - 2 in w_regrouped:
+                quantise_w_pair(turn - 2, w_regrouped[turn - 2])
 
-            multiplied = turn - QUANT_LAG
-            if multiplied in w_grouped:
-                quantise_w_pair(multiplied, w_grouped[multiplied])
-            if multiplied >= PAIRS and multiplied % PAIRS == 0:
-                b = multiplied // PAIRS - 1
-                pool_sample(b, feat_ps[b])
-            if 0 <= multiplied < len(pairs):
-                b, pair = pairs[multiplied]
+            if turn - 3 in quantised and pairs[turn - 3][1] == PAIRS - 1:
+                b = pairs[turn - 3][0]
+                pool_sample(b, feat_sums[b])
+            if turn - 2 in quantised:
+                b, pair = pairs[turn - 2]
                 if pair == 0:
-                    feat_ps[b] = [psum_feat.tile([P, CIN], F32, name="feat_ps%d" % j) for j in range(V_TILES)]
-                quantise_and_multiply(pair, h_grouped[multiplied], feat_ps[b])
+                    feat_sums[b] = [psum_feat.tile([P, CIN], F32, name="feat_ps%d" % j) for j in range(V_TILES)]
+                multiply_pair(pair, *quantised[turn - 2], feat_sums[b])
 
             if turn < PAIRS:
-                if turn % PAIRS_PER_W_LOAD == 0:
-                    w_words = load_w(turn * PAIR)
-                w_banks[turn] = transpose_w_pair(w_words, turn % PAIRS_PER_W_LOAD * PAIR)
+                w_transposed[turn] = load_and_transpose_w_pair(turn)
 
         nc.sync.dma_start(out=out.rearrange("b o c -> o b c"), in_=result[:])

@@ -18,6 +18,7 @@ PASSES = CMID // K_PASS
 V_TILES = S // P
 
 PAIR = 2
+SCALAR_PASS, VECTOR_PASS = 0, 1
 PAIRS = PASSES // PAIR
 
 FLOPS = 2 * B * S * (CIN * CMID + COUT * C8 + COUT * CIN)
@@ -47,21 +48,21 @@ def tile_occurrencepool_pa_k_kernel(tc, h_add, w_add2, b_add2, h_occ, w_occ3, ou
         bias_row = const.tile([P, CIN], BF16)
         nc.vector.memset(bias_row[:], 0.0)
 
-        w_occ_sb = const.tile([COUT, C8], BF16)
-        nc.sync.dma_start(out=w_occ_sb[:], in_=w_occ3)
-        h_occ_sb = const.tile([C8, B, S], BF16)
-        nc.sync.dma_start(out=h_occ_sb[:], in_=h_occ.rearrange("b c v -> c b v"))
-        nc.sync.dma_start(out=bias_row[0:1, :], in_=b_add2.unsqueeze(0))
-
-        bias_ps = psum_small.tile([P, CIN], F32, tag="small")
-        nc.tensor.matmul(bias_ps[:], lhsT=ones[:], rhs=bias_row[:], start=True, stop=True)
         bias_all = const.tile([P, CIN], F32)
-        nc.vector.tensor_copy(out=bias_all[:], in_=bias_ps[:])
-
-        w_occ_ps = psum_small.tile([C8, COUT], BF16, tag="small")
-        nc.tensor.transpose(w_occ_ps[:], w_occ_sb[:], ident_bf16[:])
         w_occ_t = const.tile([C8, COUT], BF16)
-        nc.vector.tensor_copy(out=w_occ_t[:], in_=w_occ_ps[:])
+        h_occ_sb = const.tile([C8, B, S], BF16)
+
+        def prepare_small_operands():
+            w_occ_sb = const.tile([COUT, C8], BF16)
+            nc.sync.dma_start(out=w_occ_sb[:], in_=w_occ3)
+            nc.sync.dma_start(out=h_occ_sb[:], in_=h_occ.rearrange("b c v -> c b v"))
+            nc.sync.dma_start(out=bias_row[0:1, :], in_=b_add2.unsqueeze(0))
+            bias_ps = psum_small.tile([P, CIN], F32, tag="small")
+            nc.tensor.matmul(bias_ps[:], lhsT=ones[:], rhs=bias_row[:], start=True, stop=True)
+            nc.vector.tensor_copy(out=bias_all[:], in_=bias_ps[:])
+            w_occ_ps = psum_small.tile([C8, COUT], BF16, tag="small")
+            nc.tensor.transpose(w_occ_ps[:], w_occ_sb[:], ident_bf16[:])
+            nc.vector.tensor_copy(out=w_occ_t[:], in_=w_occ_ps[:])
 
         table_warmer = const.tile([P, 1], F32)
         nc.scalar.activation(out=table_warmer[:], in_=ones[:, 0:1], func=mybir.ActivationFunctionType.Abs)
@@ -118,9 +119,9 @@ def tile_occurrencepool_pa_k_kernel(tc, h_add, w_add2, b_add2, h_occ, w_occ3, ou
                 in_=rows.rearrange("p t (c i) -> p c t i", i=4),
             )
 
-        def load_and_regroup(b, pair, copies):
+        def load_and_regroup(b, pair):
             h_grouped = h_groups.tile([P, PAIR, S, PACK], BF16, align_bytes=64)
-            for g, copy in enumerate(copies):
+            for g, copy in ((SCALAR_PASS, nc.scalar.copy), (VECTOR_PASS, nc.vector.tensor_copy)):
                 h_raw = h_loads.tile([P, PACK, S], BF16)
                 k0 = (pair * PAIR + g) * K_PASS
                 nc.sync.dma_start(
@@ -129,30 +130,32 @@ def tile_occurrencepool_pa_k_kernel(tc, h_add, w_add2, b_add2, h_occ, w_occ3, ou
                 regroup(copy, h_grouped[:, g], h_raw[:])
             return h_grouped
 
+        pass_order = (VECTOR_PASS, SCALAR_PASS)
+
         def quantise_h_pair(h_grouped):
-            h_codes = h_quantised.tile([P, PAIR * S], U32, align_bytes=64)
-            h_scales = h_quantised.tile([P, PAIR * S], U8, align_bytes=64)
-            nc.vector.quantize_mx(
-                out=h_codes[:].bitcast(FP8X4),
-                scales=h_scales[:],
-                in_=h_grouped[:].rearrange("p g v t -> p (g v t)"),
-            )
+            h_codes = h_quantised.tile([P, PAIR, S], U32, align_bytes=64)
+            h_scales = h_quantised.tile([P, PAIR, S], U8, align_bytes=64)
+            for g in pass_order:
+                nc.vector.quantize_mx(
+                    out=h_codes[:, g, :].bitcast(FP8X4),
+                    scales=h_scales[:, g, :],
+                    in_=h_grouped[:, g].rearrange("p v t -> p (v t)"),
+                )
             return h_codes, h_scales
 
         def multiply_pair(pair, h_codes, h_scales, feat_ps):
-            for j in range(V_TILES):
-                for g in range(PAIR):
-                    k_pass = pair * PAIR + g
-                    w_cols = slice(k_pass * CIN, (k_pass + 1) * CIN)
-                    v_cols = slice(g * S + j * P, g * S + (j + 1) * P)
+            for g in pass_order:
+                w_cols = slice((pair * PAIR + g) * CIN, (pair * PAIR + g + 1) * CIN)
+                for j in range(V_TILES):
+                    v_cols = slice(j * P, (j + 1) * P)
                     nc.tensor.matmul_mx(
                         out=feat_ps[j][:],
-                        lhsT=h_codes[:, v_cols].bitcast(FP8X4),
-                        lhsT_scale=h_scales[:, v_cols],
+                        lhsT=h_codes[:, g, v_cols].bitcast(FP8X4),
+                        lhsT_scale=h_scales[:, g, v_cols],
                         rhs=w_codes[:, w_cols].bitcast(FP8X4),
                         rhs_scale=w_scales[:, w_cols],
-                        start=(k_pass == 0),
-                        stop=(k_pass == PASSES - 1),
+                        start=(pair == 0 and g == pass_order[0]),
+                        stop=(pair == PAIRS - 1 and g == pass_order[-1]),
                     )
 
         result = const.tile([COUT, B, CIN], F32)
@@ -192,19 +195,16 @@ def tile_occurrencepool_pa_k_kernel(tc, h_add, w_add2, b_add2, h_occ, w_occ3, ou
             nc.scalar.mul(out=result[:, b, :], in_=out_ps[:], mul=1.0 / S)
 
         pairs = [(b, pair) for b in range(B) for pair in range(PAIRS)]
-        last = len(pairs) - 1
         regrouped = {}
         quantised = {}
         w_transposed = {}
         w_regrouped = {}
         feat_sums = {}
         for turn in range(len(pairs) + 3):
-            if turn <= last:
-                first_copy = nc.vector.tensor_copy if turn == 0 else nc.scalar.copy
-                second_copy = nc.scalar.copy if turn == last else nc.vector.tensor_copy
-                regrouped[turn] = load_and_regroup(*pairs[turn], (first_copy, second_copy))
-            if turn == 0:
-                for b in range(B):
+            if turn < len(pairs):
+                b, pair = pairs[turn]
+                regrouped[turn] = load_and_regroup(b, pair)
+                if pair == PAIRS - 1:
                     occurrence_maps(b)
             if turn - 1 in w_transposed:
                 w_regrouped[turn - 1] = regroup_w_pair(w_transposed[turn - 1])
@@ -224,5 +224,7 @@ def tile_occurrencepool_pa_k_kernel(tc, h_add, w_add2, b_add2, h_occ, w_occ3, ou
 
             if turn < PAIRS:
                 w_transposed[turn] = load_and_transpose_w_pair(turn)
+            if turn == 0:
+                prepare_small_operands()
 
         nc.sync.dma_start(out=out.rearrange("b o c -> o b c"), in_=result[:])

@@ -18,7 +18,7 @@ PASSES = CMID // K_PASS
 V_TILES = S // P
 
 PAIR = 2
-SCALAR_PASS, VECTOR_PASS = 0, 1
+SCALAR_VOXELS = (248, 264)
 PAIRS = PASSES // PAIR
 
 FLOPS = 2 * B * S * (CIN * CMID + COUT * C8 + COUT * CIN)
@@ -113,24 +113,26 @@ def tile_occurrencepool_pa_k_kernel(tc, h_add, w_add2, b_add2, h_occ, w_occ3, ou
                 out=w_codes[:, cols].bitcast(FP8X4), scales=w_scales[:, cols], in_=w_grouped[:]
             )
 
-        def regroup(copy, grouped, rows):
+        def regroup(copy, grouped, rows, voxels):
             copy(
-                out=grouped.rearrange("p (c i) t -> p c t i", i=4),
-                in_=rows.rearrange("p t (c i) -> p c t i", i=4),
+                out=grouped[:, voxels, :].rearrange("p (c i) t -> p c t i", i=4),
+                in_=rows[:, :, voxels].rearrange("p t (c i) -> p c t i", i=4),
             )
 
         def load_and_regroup(b, pair):
             h_grouped = h_groups.tile([P, PAIR, S, PACK], BF16, align_bytes=64)
-            for g, copy in ((SCALAR_PASS, nc.scalar.copy), (VECTOR_PASS, nc.vector.tensor_copy)):
+            cut = SCALAR_VOXELS[b]
+            for g in range(PAIR):
                 h_raw = h_loads.tile([P, PACK, S], BF16)
                 k0 = (pair * PAIR + g) * K_PASS
                 nc.sync.dma_start(
                     out=h_raw[:], in_=h_add[b, k0 : k0 + K_PASS, :].rearrange("(p t) v -> p t v", t=PACK)
                 )
-                regroup(copy, h_grouped[:, g], h_raw[:])
+                regroup(nc.scalar.copy, h_grouped[:, g], h_raw[:], slice(0, cut))
+                regroup(nc.vector.tensor_copy, h_grouped[:, g], h_raw[:], slice(cut, S))
             return h_grouped
 
-        pass_order = (VECTOR_PASS, SCALAR_PASS)
+        pass_order = (0, 1)
 
         def quantise_h_pair(h_grouped):
             h_codes = h_quantised.tile([P, PAIR, S], U32, align_bytes=64)

@@ -18,7 +18,7 @@ PASSES = CMID // K_PASS
 V_TILES = S // P
 
 PAIR = 2
-SCALAR_VOXELS = (248, 264)
+SCALAR_VOXELS = (240, 256)
 PAIRS = PASSES // PAIR
 
 FLOPS = 2 * B * S * (CIN * CMID + COUT * C8 + COUT * CIN)
@@ -115,8 +115,8 @@ def tile_occurrencepool_pa_k_kernel(tc, h_add, w_add2, b_add2, h_occ, w_occ3, ou
 
         def regroup(copy, grouped, rows, voxels):
             copy(
-                out=grouped[:, voxels, :].rearrange("p (c i) t -> p c t i", i=4),
-                in_=rows[:, :, voxels].rearrange("p t (c i) -> p c t i", i=4),
+                out=grouped[:, voxels, :].rearrange("p (c i) t -> p c t i", i=8),
+                in_=rows[:, :, voxels].rearrange("p t (c i) -> p c t i", i=8),
             )
 
         def load_and_regroup(b, pair):

@@ -134,14 +134,21 @@ def tile_occurrencepool_pa_k_kernel(tc, h_add, w_add2, b_add2, h_occ, w_occ3, ou
 
         pass_order = (0, 1)
 
-        def quantise_h_pair(h_grouped):
+        def quantise_h_pair(h_grouped, by_pass):
             h_codes = h_quantised.tile([P, PAIR, S], U32, align_bytes=64)
             h_scales = h_quantised.tile([P, PAIR, S], U8, align_bytes=64)
-            for g in pass_order:
+            if by_pass:
+                for g in pass_order:
+                    nc.vector.quantize_mx(
+                        out=h_codes[:, g, :].bitcast(FP8X4),
+                        scales=h_scales[:, g, :],
+                        in_=h_grouped[:, g].rearrange("p v t -> p (v t)"),
+                    )
+            else:
                 nc.vector.quantize_mx(
-                    out=h_codes[:, g, :].bitcast(FP8X4),
-                    scales=h_scales[:, g, :],
-                    in_=h_grouped[:, g].rearrange("p v t -> p (v t)"),
+                    out=h_codes[:].rearrange("p g v -> p (g v)").bitcast(FP8X4),
+                    scales=h_scales[:].rearrange("p g v -> p (g v)"),
+                    in_=h_grouped[:].rearrange("p g v t -> p (g v t)"),
                 )
             return h_codes, h_scales
 
@@ -211,7 +218,7 @@ def tile_occurrencepool_pa_k_kernel(tc, h_add, w_add2, b_add2, h_occ, w_occ3, ou
             if turn - 1 in w_transposed:
                 w_regrouped[turn - 1] = regroup_w_pair(w_transposed[turn - 1])
             if turn - 1 in regrouped:
-                quantised[turn - 1] = quantise_h_pair(regrouped[turn - 1])
+                quantised[turn - 1] = quantise_h_pair(regrouped[turn - 1], turn == len(pairs))
             if turn - 2 in w_regrouped:
                 quantise_w_pair(turn - 2, w_regrouped[turn - 2])
 

from contextlib import ExitStack

import concourse.mybir as mybir
from concourse.masks import make_identity

F32 = mybir.dt.float32
BF16 = mybir.dt.bfloat16
U32 = mybir.dt.uint32
U8 = mybir.dt.uint8
FP8X4 = mybir.dt.float8_e4m3fn_x4

B, CIN, CMID, C8, COUT, S = 2, 128, 16384, 128, 128, 512

P = 128
PACK = 4
K_PASS = P * PACK
PASSES = CMID // K_PASS
V_TILES = S // P

PAIR = 2
SCALAR_VOXELS = (240, 256)
PAIRS = PASSES // PAIR

FLOPS = 2 * B * S * (CIN * CMID + COUT * C8 + COUT * CIN)


def tile_occurrencepool_pa_k_kernel(tc, h_add, w_add2, b_add2, h_occ, w_occ3, out):
    nc = tc.nc
    with ExitStack() as ctx:
        const = ctx.enter_context(tc.tile_pool(name="const", bufs=1))
        w_loads = ctx.enter_context(tc.tile_pool(name="w_loads", bufs=4))
        w_stage = ctx.enter_context(tc.tile_pool(name="w_stage", bufs=3))
        h_loads = ctx.enter_context(tc.tile_pool(name="h_loads", bufs=16))
        h_groups = ctx.enter_context(tc.tile_pool(name="h_groups", bufs=4))
        h_quantised = ctx.enter_context(tc.tile_pool(name="h_quantised", bufs=4))
        pooling = ctx.enter_context(tc.tile_pool(name="pooling", bufs=2))
        psum_feat = ctx.enter_context(tc.psum_pool(name="psum_feat", bufs=1))
        psum_wt = ctx.enter_context(tc.psum_pool(name="psum_wt", bufs=2))
        psum_small = ctx.enter_context(tc.psum_pool(name="psum_small", bufs=2))
        ctx.enter_context(tc.manual_schedule())

        ident_bf16 = const.tile([P, P], BF16)
        make_identity(nc, ident_bf16[:])
        ident_f32 = const.tile([P, P], F32)
        make_identity(nc, ident_f32[:])
        ones = const.tile([P, P], BF16)
        nc.vector.memset(ones[:], 1.0)
        bias_row = const.tile([P, CIN], BF16)
        nc.vector.memset(bias_row[:], 0.0)

        bias_all = const.tile([P, CIN], F32)
        w_occ_t = const.tile([C8, COUT], BF16)
        h_occ_sb = const.tile([C8, B, S], BF16)

        def prepare_small_operands():
            w_occ_sb = const.tile([COUT, C8], BF16)
            nc.sync.dma_start(out=w_occ_sb[:], in_=w_occ3)
            nc.sync.dma_start(out=h_occ_sb[:], in_=h_occ.rearrange("b c v -> c b v"))
            nc.sync.dma_start(out=bias_row[0:1, :], in_=b_add2.unsqueeze(0))
            bias_ps = psum_small.tile([P, CIN], F32, tag="small")
            nc.tensor.matmul(bias_ps[:], lhsT=ones[:], rhs=bias_row[:], start=True, stop=True)
            nc.vector.tensor_copy(out=bias_all[:], in_=bias_ps[:])
            w_occ_ps = psum_small.tile([C8, COUT], BF16, tag="small")
            nc.tensor.transpose(w_occ_ps[:], w_occ_sb[:], ident_bf16[:])
            nc.vector.tensor_copy(out=w_occ_t[:], in_=w_occ_ps[:])

        table_warmer = const.tile([P, 1], F32)
        nc.scalar.activation(out=table_warmer[:], in_=ones[:, 0:1], func=mybir.ActivationFunctionType.Abs)

        occ_grouped = const.tile([P, B, COUT, PACK], BF16, align_bytes=64)

        def occurrence_maps(b):
            occ_ps = psum_small.tile([P, V_TILES, COUT], F32, tag="small")
            for t in range(V_TILES):
                nc.tensor.matmul(
                    occ_ps[:, t, :],
                    lhsT=h_occ_sb[:, b, t * P : (t + 1) * P],
                    rhs=w_occ_t[:],
                    start=True,
                    stop=True,
                )
            nc.scalar.activation(
                out=occ_grouped[:, b],
                in_=occ_ps[:].rearrange("p t o -> p o t"),
                func=mybir.ActivationFunctionType.Abs,
            )

        w_codes = const.tile([P, PASSES * CIN], U32, align_bytes=64)
        w_scales = const.tile([P, PASSES * CIN], U8, align_bytes=64)

        def load_and_transpose_w_pair(pair):
            w_raw = w_loads.tile([CIN, PAIR * K_PASS], BF16)
            k0 = pair * PAIR * K_PASS
            nc.sync.dma_start(out=w_raw[:], in_=w_add2[:, k0 : k0 + PAIR * K_PASS])
            w_words = w_raw[:].bitcast(F32).rearrange("c (g p u) -> c g u p", p=P, u=2)
            w_bank = psum_wt.tile([P, PAIR, 2, CIN], F32)
            for g in range(PAIR):
                for u in range(2):
                    nc.tensor.transpose(w_bank[:, g, u, :], w_words[:, g, u, :], ident_f32[:])
            return w_bank

        def regroup_w_pair(w_bank):
            w_grouped = w_stage.tile([P, PAIR * CIN * PACK], BF16, align_bytes=64)
            nc.scalar.copy(
                out=w_grouped[:].bitcast(F32).rearrange("p (g c u) -> p g c u", c=CIN, u=2),
                in_=w_bank[:].rearrange("p g u c -> p g c u"),
            )
            return w_grouped

        def quantise_w_pair(pair, w_grouped):
            cols = slice(pair * PAIR * CIN, (pair + 1) * PAIR * CIN)
            nc.vector.quantize_mx(
                out=w_codes[:, cols].bitcast(FP8X4), scales=w_scales[:, cols], in_=w_grouped[:]
            )

        def regroup(copy, grouped, rows, voxels):
            copy(
                out=grouped[:, voxels, :].rearrange("p (c i) t -> p c t i", i=8),
                in_=rows[:, :, voxels].rearrange("p t (c i) -> p c t i", i=8),
            )

        def load_and_regroup(b, pair):
            h_grouped = h_groups.tile([P, PAIR, S, PACK], BF16, align_bytes=64)
            cut = SCALAR_VOXELS[b]
            for g in range(PAIR):
                h_raw = h_loads.tile([P, PACK, S], BF16)
                k0 = (pair * PAIR + g) * K_PASS
                nc.sync.dma_start(
                    out=h_raw[:], in_=h_add[b, k0 : k0 + K_PASS, :].rearrange("(p t) v -> p t v", t=PACK)
                )
                regroup(nc.scalar.copy, h_grouped[:, g], h_raw[:], slice(0, cut))
                regroup(nc.vector.tensor_copy, h_grouped[:, g], h_raw[:], slice(cut, S))
            return h_grouped

        pass_order = (0, 1)

        def quantise_h_pair(h_grouped, by_pass):
            h_codes = h_quantised.tile([P, PAIR, S], U32, align_bytes=64)
            h_scales = h_quantised.tile([P, PAIR, S], U8, align_bytes=64)
            if by_pass:
                for g in pass_order:
                    nc.vector.quantize_mx(
                        out=h_codes[:, g, :].bitcast(FP8X4),
                        scales=h_scales[:, g, :],
                        in_=h_grouped[:, g].rearrange("p v t -> p (v t)"),
                    )
            else:
                nc.vector.quantize_mx(
                    out=h_codes[:].rearrange("p g v -> p (g v)").bitcast(FP8X4),
                    scales=h_scales[:].rearrange("p g v -> p (g v)"),
                    in_=h_grouped[:].rearrange("p g v t -> p (g v t)"),
                )
            return h_codes, h_scales

        def multiply_pair(pair, h_codes, h_scales, feat_ps):
            for g in pass_order:
                w_cols = slice((pair * PAIR + g) * CIN, (pair * PAIR + g + 1) * CIN)
                for j in range(V_TILES):
                    v_cols = slice(j * P, (j + 1) * P)
                    nc.tensor.matmul_mx(
                        out=feat_ps[j][:],
                        lhsT=h_codes[:, g, v_cols].bitcast(FP8X4),
                        lhsT_scale=h_scales[:, g, v_cols],
                        rhs=w_codes[:, w_cols].bitcast(FP8X4),
                        rhs_scale=w_scales[:, w_cols],
                        start=(pair == 0 and g == pass_order[0]),
                        stop=(pair == PAIRS - 1 and g == pass_order[-1]),
                    )

        result = const.tile([COUT, B, CIN], F32)

        def pool_sample(b, feat_ps):
            occ_codes = pooling.tile([P, COUT], U32, align_bytes=64)
            occ_scales = pooling.tile([P, COUT], U8, align_bytes=64)
            nc.vector.quantize_mx(
                out=occ_codes[:].bitcast(FP8X4),
                scales=occ_scales[:],
                in_=occ_grouped[:, b].rearrange("p o t -> p (o t)"),
            )
            feat_rows = pooling.tile([P, V_TILES, CIN], BF16)
            for j in range(V_TILES):
                nc.vector.tensor_tensor(
                    out=feat_rows[:, j, :], in0=feat_ps[j][:], in1=bias_all[:], op=mybir.AluOpType.add
                )
            feat_grouped = pooling.tile([P, CIN, PACK], BF16, align_bytes=64)
            nc.vector.tensor_copy(out=feat_grouped[:], in_=feat_rows[:].rearrange("p t c -> p c t"))
            feat_codes = pooling.tile([P, CIN], U32, align_bytes=64)
            feat_scales = pooling.tile([P, CIN], U8, align_bytes=64)
            nc.vector.quantize_mx(
                out=feat_codes[:].bitcast(FP8X4),
                scales=feat_scales[:],
                in_=feat_grouped[:].rearrange("p c t -> p (c t)"),
            )
            out_ps = psum_small.tile([COUT, CIN], F32, tag="small")
            nc.tensor.matmul_mx(
                out=out_ps[:],
                lhsT=occ_codes[:].bitcast(FP8X4),
                lhsT_scale=occ_scales[:],
                rhs=feat_codes[:].bitcast(FP8X4),
                rhs_scale=feat_scales[:],
                start=True,
                stop=True,
            )
            nc.scalar.mul(out=result[:, b, :], in_=out_ps[:], mul=1.0 / S)

        pairs = [(b, pair) for b in range(B) for pair in range(PAIRS)]
        regrouped = {}
        quantised = {}
        w_transposed = {}
        w_regrouped = {}
        feat_sums = {}
        for turn in range(len(pairs) + 3):
            if turn < len(pairs):
                b, pair = pairs[turn]
                regrouped[turn] = load_and_regroup(b, pair)
                if pair == PAIRS - 1:
                    occurrence_maps(b)
            if turn - 1 in w_transposed:
                w_regrouped[turn - 1] = regroup_w_pair(w_transposed[turn - 1])
            if turn - 1 in regrouped:
                quantised[turn - 1] = quantise_h_pair(regrouped[turn - 1], turn == len(pairs))
            if turn - 2 in w_regrouped:
                quantise_w_pair(turn - 2, w_regrouped[turn - 2])

            if turn - 3 in quantised and pairs[turn - 3][1] == PAIRS - 1:
                b = pairs[turn - 3][0]
                pool_sample(b, feat_sums[b])
            if turn - 2 in quantised:
                b, pair = pairs[turn - 2]
                if pair == 0:
                    feat_sums[b] = [psum_feat.tile([P, CIN], F32, name="feat_ps%d" % j) for j in range(V_TILES)]
                multiply_pair(pair, *quantised[turn - 2], feat_sums[b])

            if turn < PAIRS:
                w_transposed[turn] = load_and_transpose_w_pair(turn)
            if turn == 0:
                prepare_small_operands()

        nc.sync.dma_start(out=out.rearrange("b o c -> o b c"), in_=result[:])
